import numpy as np
import ml_dtypes


def mxq(x, axis, fmt="e4m3"):
    dtype, down = {"e4m3": (ml_dtypes.float8_e4m3fn, 7), "e5m2": (ml_dtypes.float8_e5m2, 14)}[fmt]
    v = np.moveaxis(np.asarray(x, np.float32).astype(ml_dtypes.bfloat16).astype(np.float64), axis, -1)
    blocks = v.reshape(v.shape[:-1] + (-1, 32))
    amax = np.abs(blocks).max(-1, keepdims=True)
    byte = np.maximum(np.where(amax > 0, np.frexp(amax)[1] - 1 + 127, 0) - down, 1)
    scale = np.exp2(byte - 127.0)
    codes = (blocks / scale).astype(np.float32).astype(dtype).astype(np.float64)
    return np.moveaxis((codes * scale).reshape(v.shape), -1, axis)


WIDE = False


def mx_kscale(k):
    if not WIDE:
        return np.ones(k)
    levels = np.array([10, -10, 5, -5, 0])
    if k % 512:
        return np.exp2(np.random.permutation(np.resize(levels, k // 32))).repeat(32)
    a = np.empty((k // 512, 16))
    for p in range(k // 512):
        a[p, :8] = np.random.permutation(np.resize(levels, 8))
        for g in range(8):
            far = levels[np.abs(levels - a[p, g]) >= 10]
            a[p, g + 8] = far[np.random.randint(len(far))]
    return np.exp2(a.ravel()).repeat(32)


BF16 = ml_dtypes.bfloat16


def bf(x):
    return np.asarray(x, np.float32).astype(BF16)


def f64(x):
    return np.asarray(x).astype(np.float64)


B, N, D, NFF = 128, 1024, 8, 1024
KI = D * N
ALPHA = 0.95
RHO = 0.9
BETA = 1.8
TH = 1.0
P = 0.1
GAP = 0.0625


def spikes(shape):
    return (np.random.random_sample(shape) < P) * (1.0 + 0.25 * np.random.standard_normal(shape))


def setup_inputs():
    s = mx_kscale(KI).reshape(D, N)
    u = mx_kscale(NFF)
    a = bf(np.random.random_sample((B, N)))
    theta = TH + BETA * f64(a)
    d = 1.0 + 1.5 * np.random.standard_normal((B, N)) - theta
    V = bf(theta + d + GAP * np.sign(d))
    return {"FF": bf(spikes((B, NFF)) * u),
            "V": V,
            "a": a,
            "Xd": bf(spikes((D, B, N)) * s[:, None, :]),
            "W_int": bf(np.random.standard_normal((D, N, N)) * 0.8 / np.sqrt(P * KI) / s[:, :, None]),
            "W_ff": bf(np.random.standard_normal((NFF, N)) * 0.8 / np.sqrt(P * NFF) / u[:, None])}


def core(FF, V, a, Xd, W_int, W_ff):
    FF, V, a, Xd, W_int, W_ff = f64(FF), f64(V), f64(a), f64(Xd), f64(W_int), f64(W_ff)
    theta = TH + BETA * a
    X = (V - theta > 0).astype(np.float64)
    xq = mxq(Xd.transpose(1, 0, 2).reshape(B, KI), 1, "e4m3")
    wq = mxq(W_int.reshape(KI, N), 0, "e4m3")
    I_int = xq @ wq
    I_ff = mxq(FF, 1, "e4m3") @ mxq(W_ff, 0, "e4m3")
    current = I_int + I_ff
    V_new = ALPHA * V * (1.0 - X) + current
    a_new = RHO * a + X
    return np.stack([X, V_new, a_new])


def e4m3fn_bytes(y):
    return np.clip(np.asarray(y, np.float64), -448.0, 448.0).astype(np.float32).astype(ml_dtypes.float8_e4m3fn).view(np.uint8)


Y_SCALE = 190.0


def reference(FF, V, a, Xd, W_int, W_ff):
    out = core(FF, V, a, Xd, W_int, W_ff)
    return out, e4m3fn_bytes(out * Y_SCALE)

@@ -1,0 +1,227 @@
+from contextlib import ExitStack
+
+import concourse.mybir as mybir
+from concourse.masks import make_identity
+
+FLOPS = 2 * 128 * 9216 * 1024
+
+F32 = mybir.dt.float32
+BF16 = mybir.dt.bfloat16
+U32 = mybir.dt.uint32
+U8 = mybir.dt.uint8
+FP8X4 = mybir.dt.float8_e4m3fn_x4
+FP8 = mybir.dt.float8_e4m3fn
+ALU = mybir.AluOpType
+ACT = mybir.ActivationFunctionType
+
+P = 128
+N = 1024
+HALF = 512
+GROUPS = 9
+PASSES = 18
+RAW_BUFS = 12
+Y_SCALE = 190.0
+
+
+def tile_snn_kernel(tc, FF, V, a, Xd, W_int, W_ff, out_0, out_1):
+    nc = tc.nc
+
+    def w_rows(i):
+        s, h = divmod(i, 2)
+        src = W_int[s] if s < 8 else W_ff
+        return src[HALF * h : HALF * (h + 1), :].rearrange("(p j) w -> p j w", j=4)
+
+    def x_rows(s):
+        return Xd[s] if s < 8 else FF
+
+    with ExitStack() as ctx:
+        keep = ctx.enter_context(tc.tile_pool(name="keep", bufs=1))
+        rawp = ctx.enter_context(tc.tile_pool(name="rawp", bufs=RAW_BUFS))
+        grp = ctx.enter_context(tc.tile_pool(name="grp", bufs=3))
+        accp = ctx.enter_context(tc.psum_pool(name="accp", bufs=1))
+        xtp = ctx.enter_context(tc.psum_pool(name="xtp", bufs=2))
+
+        ident = keep.tile([P, P], F32, name="ident")
+        make_identity(nc, ident[:])
+        warm_in = keep.tile([P, 8], F32, name="warm_in")
+        warm_out = keep.tile([P, 8], F32, name="warm_out")
+        nc.gpsimd.memset(warm_in[:], 0.0)
+        nc.scalar.activation(out=warm_out[:], in_=warm_in[:], func=ACT.Copy)
+
+        x_sb = keep.tile([P, GROUPS, N], BF16, name="x_sb")
+        x_codes = keep.tile([P, PASSES, P], U32, name="x_codes", align_bytes=64)
+        x_scales = keep.tile([P, PASSES, P], U8, name="x_scales", align_bytes=64)
+        a_sb = keep.tile([P, N], BF16, name="a_sb")
+        v_sb = keep.tile([P, N], BF16, name="v_sb")
+        t_sb = keep.tile([P, N], F32, name="t_sb")
+        x_out = keep.tile([P, N], F32, name="x_out")
+        a_out = keep.tile([P, N], F32, name="a_out")
+        v_keep = keep.tile([P, N], F32, name="v_keep")
+        v_out = keep.tile([P, N], F32, name="v_out")
+        x_f8 = keep.tile([P, N], FP8, name="x_f8")
+        a_f8 = keep.tile([P, N], FP8, name="a_f8")
+        v_f8 = keep.tile([P, N], FP8, name="v_f8")
+        acc = [accp.tile([P, HALF], F32, name="acc%d" % c) for c in range(2)]
+
+        raw = {}
+        grouped = {}
+        codes = {}
+        scales = {}
+
+        def load_w(i, chunks=1):
+            raw[i] = rawp.tile([P, 4, N], BF16, name="raw")
+            step = N // chunks
+            order = list(range(chunks))
+            if chunks == 4:
+                order = [0, 2, 1, 3]
+            for c in order:
+                cols = slice(c * step, (c + 1) * step)
+                nc.sync.dma_start(out=raw[i][:, :, cols], in_=w_rows(i)[:, :, cols])
+
+        def load_x(s):
+            nc.sync.dma_start(out=x_sb[:, s, :], in_=x_rows(s))
+
+        def alloc_grouped(i):
+            for c in range(2):
+                grouped[i, c] = grp.tile([P, HALF, 4], BF16, name="g%d" % c, align_bytes=64)
+
+        def copy_cols(eng, i, c0, c1):
+            c = c0 // HALF
+            dst = grouped[i, c][:, c0 - c * HALF : c1 - c * HALF, :]
+            src = raw[i][:, :, c0:c1].rearrange("p j w -> p w j")
+            if eng == "v":
+                nc.vector.tensor_copy(out=dst, in_=src)
+            else:
+                nc.scalar.copy(out=dst, in_=src)
+
+        def quant(i, c):
+            codes[i, c] = grp.tile([P, HALF], U32, name="c%d" % c, align_bytes=64)
+            scales[i, c] = grp.tile([P, HALF], U8, name="s%d" % c, align_bytes=64)
+            nc.vector.quantize_mx(
+                out=codes[i, c][:].bitcast(FP8X4),
+                scales=scales[i, c][:],
+                in_=grouped[i, c][:].rearrange("p w j -> p (w j)"),
+            )
+
+        def mm(i, c):
+            nc.tensor.matmul_mx(
+                out=acc[c][:],
+                lhsT=x_codes[:, i, :].bitcast(FP8X4),
+                lhsT_scale=x_scales[:, i, :],
+                rhs=codes[i, c][:].bitcast(FP8X4),
+                rhs_scale=scales[i, c][:],
+                start=(i == 0),
+                stop=(i == PASSES - 1),
+            )
+
+        xt = {}
+        gx = {}
+
+        def xpose(s):
+            words = x_sb[:, s, :].bitcast(F32)
+            xt[s] = xtp.tile([P, 2, 2, P], F32, name="xt")
+            for h in range(2):
+                for u in range(2):
+                    nc.tensor.transpose(
+                        xt[s][:, h, u, :], words[:, 256 * h + u : 256 * (h + 1) : 2], ident[:]
+                    )
+
+        def xcopy(s):
+            gx[s] = grp.tile([P, 2, P, 2], F32, name="gx", align_bytes=64)
+            nc.scalar.copy(out=gx[s][:], in_=xt[s][:].rearrange("p h u r -> p h r u"))
+
+        def xquant(s):
+            nc.vector.quantize_mx(
+                out=x_codes[:, 2 * s : 2 * s + 2, :].rearrange("p a m -> p (a m)").bitcast(FP8X4),
+                scales=x_scales[:, 2 * s : 2 * s + 2, :].rearrange("p a m -> p (a m)"),
+                in_=gx[s][:].rearrange("p h r u -> p (h r u)").bitcast(BF16),
+            )
+
+        load_w(0, chunks=4)
+        load_x(0)
+        load_w(1)
+        load_x(1)
+        load_w(2)
+        nc.sync.dma_start(out=a_sb[:], in_=a)
+        nc.sync.dma_start(out=v_sb[:], in_=V)
+        load_w(3)
+        for i in range(4, RAW_BUFS):
+            if i % 2 == 0:
+                load_x(i // 2)
+            load_w(i)
+
+        alloc_grouped(0)
+        copy_cols("v", 0, 0, 256)
+        copy_cols("s", 0, 512, 768)
+        copy_cols("v", 0, 256, 512)
+        copy_cols("s", 0, 768, 1024)
+        xpose(0)
+        xcopy(0)
+        xquant(0)
+
+        def elementwise(step):
+            if step == 2:
+                nc.vector.scalar_tensor_tensor(
+                    out=t_sb[:], in0=a_sb[:], scalar=-1.8, in1=v_sb[:], op0=ALU.mult, op1=ALU.add
+                )
+            if step == 3:
+                nc.vector.tensor_scalar(
+                    out=x_out[:], in0=t_sb[:], scalar1=1.0, scalar2=None, op0=ALU.is_gt
+                )
+                nc.sync.dma_start(out=out_0[0], in_=x_out[:])
+            if step == 4:
+                nc.vector.scalar_tensor_tensor(
+                    out=a_out[:], in0=a_sb[:], scalar=0.9, in1=x_out[:], op0=ALU.mult, op1=ALU.add
+                )
+                nc.sync.dma_start(out=out_0[2], in_=a_out[:])
+                nc.scalar.activation(
+                    out=x_f8[:], in_=x_out[:], func=ACT.Copy, scale=Y_SCALE, saturate=False
+                )
+                nc.sync.dma_start(out=out_1[0], in_=x_f8[:].bitcast(U8))
+            if step == 5:
+                nc.vector.scalar_tensor_tensor(
+                    out=v_keep[:], in0=t_sb[:], scalar=1.0, in1=v_sb[:], op0=ALU.is_le, op1=ALU.mult
+                )
+                nc.scalar.activation(
+                    out=a_f8[:], in_=a_out[:], func=ACT.Copy, scale=Y_SCALE, saturate=False
+                )
+                nc.sync.dma_start(out=out_1[2], in_=a_f8[:].bitcast(U8))
+
+        for i in range(PASSES):
+            nxt = i + 1
+            if nxt < PASSES:
+                alloc_grouped(nxt)
+                if nxt == PASSES - 1:
+                    copy_cols("v", nxt, 0, 512)
+                    copy_cols("s", nxt, 512, 768)
+                    copy_cols("v", nxt, 768, 1024)
+                else:
+                    copy_cols("v", nxt, 0, 512)
+                    copy_cols("s", nxt, 512, 1024)
+                if nxt + RAW_BUFS - 1 < PASSES:
+                    j = nxt + RAW_BUFS - 1
+                    if j % 2 == 0:
+                        load_x(j // 2)
+                    load_w(j)
+            if i % 2 == 0 and i // 2 + 1 < GROUPS:
+                xpose(i // 2 + 1)
+                xcopy(i // 2 + 1)
+            quant(i, 0)
+            mm(i, 0)
+            quant(i, 1)
+            mm(i, 1)
+            if i % 2 == 1 and i // 2 + 1 < GROUPS:
+                xquant(i // 2 + 1)
+            elementwise(i)
+
+        for c in range(2):
+            cols = slice(c * HALF, (c + 1) * HALF)
+            nc.vector.scalar_tensor_tensor(
+                out=v_out[:, cols], in0=v_keep[:, cols], scalar=0.95, in1=acc[c][:],
+                op0=ALU.mult, op1=ALU.add,
+            )
+            nc.sync.dma_start(out=out_0[1][:, cols], in_=v_out[:, cols])
+            nc.scalar.activation(
+                out=v_f8[:, cols], in_=v_out[:, cols], func=ACT.Copy, scale=Y_SCALE, saturate=False
+            )
+            nc.sync.dma_start(out=out_1[1][:, cols], in_=v_f8[:, cols].bitcast(U8))

@@ -87,8 +87,10 @@ def tile_snn_kernel(tc, FF, V, a, Xd, W_int, W_ff, out_0, out_1):
 
         def copy_cols(eng, i, c0, c1):
             c = c0 // HALF
-            dst = grouped[i, c][:, c0 - c * HALF : c1 - c * HALF, :]
-            src = raw[i][:, :, c0:c1].rearrange("p j w -> p w j")
+            dst = grouped[i, c][:, c0 - c * HALF : c1 - c * HALF, :].rearrange(
+                "p (c i) t -> p c t i", i=4
+            )
+            src = raw[i][:, :, c0:c1].rearrange("p t (c i) -> p c t i", i=4)
             if eng == "v":
                 nc.vector.tensor_copy(out=dst, in_=src)
             else:

@@ -21,6 +21,11 @@ GROUPS = 9
 PASSES = 18
 RAW_BUFS = 12
 Y_SCALE = 190.0
+CV = 528
+CV_PE = 488
+CV_LAST = 512
+PE_FROM = 11
+PE_COLS = 256
 
 
 def tile_snn_kernel(tc, FF, V, a, Xd, W_int, W_ff, out_0, out_1):
@@ -40,9 +45,13 @@ def tile_snn_kernel(tc, FF, V, a, Xd, W_int, W_ff, out_0, out_1):
         grp = ctx.enter_context(tc.tile_pool(name="grp", bufs=3))
         accp = ctx.enter_context(tc.psum_pool(name="accp", bufs=1))
         xtp = ctx.enter_context(tc.psum_pool(name="xtp", bufs=2))
+        pwp = ctx.enter_context(tc.psum_pool(name="pwp", bufs=3))
+        ctx.enter_context(tc.manual_schedule())
 
         ident = keep.tile([P, P], F32, name="ident")
         make_identity(nc, ident[:])
+        ident_bf = keep.tile([P, P], BF16, name="ident_bf")
+        make_identity(nc, ident_bf[:])
         warm_in = keep.tile([P, 8], F32, name="warm_in")
         warm_out = keep.tile([P, 8], F32, name="warm_out")
         nc.gpsimd.memset(warm_in[:], 0.0)
@@ -67,57 +76,67 @@ def tile_snn_kernel(tc, FF, V, a, Xd, W_int, W_ff, out_0, out_1):
         grouped = {}
         codes = {}
         scales = {}
+        xt = {}
+        gx = {}
 
-        def load_w(i, chunks=1):
+        def load_w(i, pieces=((0, N),)):
             raw[i] = rawp.tile([P, 4, N], BF16, name="raw")
-            step = N // chunks
-            order = list(range(chunks))
-            if chunks == 4:
-                order = [0, 2, 1, 3]
-            for c in order:
-                cols = slice(c * step, (c + 1) * step)
-                nc.sync.dma_start(out=raw[i][:, :, cols], in_=w_rows(i)[:, :, cols])
+            for c0, c1 in pieces:
+                nc.sync.dma_start(out=raw[i][:, :, c0:c1], in_=w_rows(i)[:, :, c0:c1])
+
+        def load_w_piece(i, c0, c1):
+            nc.sync.dma_start(out=raw[i][:, :, c0:c1], in_=w_rows(i)[:, :, c0:c1])
 
         def load_x(s):
             nc.sync.dma_start(out=x_sb[:, s, :], in_=x_rows(s))
 
-        def alloc_grouped(i):
-            for c in range(2):
-                grouped[i, c] = grp.tile([P, HALF, 4], BF16, name="g%d" % c, align_bytes=64)
-
         def copy_cols(eng, i, c0, c1):
-            c = c0 // HALF
-            dst = grouped[i, c][:, c0 - c * HALF : c1 - c * HALF, :].rearrange(
-                "p (c i) t -> p c t i", i=4
-            )
+            dst = grouped[i][:, c0:c1, :].rearrange("p (c i) t -> p c t i", i=4)
             src = raw[i][:, :, c0:c1].rearrange("p t (c i) -> p c t i", i=4)
             if eng == "v":
                 nc.vector.tensor_copy(out=dst, in_=src)
             else:
                 nc.scalar.copy(out=dst, in_=src)
 
-        def quant(i, c):
-            codes[i, c] = grp.tile([P, HALF], U32, name="c%d" % c, align_bytes=64)
-            scales[i, c] = grp.tile([P, HALF], U8, name="s%d" % c, align_bytes=64)
+        pw = {}
+
+        def pe_interleave(i):
+            pw[i] = pwp.tile([P, PE_COLS, 4], BF16, name="pw")
+            for j in (0, 2):
+                nc.tensor.matmul(
+                    out=pw[i][:, :, j : j + 2],
+                    lhsT=ident_bf[:],
+                    rhs=raw[i][:, j : j + 2, N - PE_COLS : N].rearrange("p j c -> p c j"),
+                    start=True, stop=True,
+                )
+
+        def pe_collect(i):
+            nc.scalar.copy(out=grouped[i][:, N - PE_COLS : N, :], in_=pw[i][:])
+
+        def alloc_pass(i):
+            grouped[i] = grp.tile([P, N, 4], BF16, name="g", align_bytes=64)
+
+        def quant(i, c0, c1):
+            if c0 == 0:
+                codes[i] = grp.tile([P, N], U32, name="c", align_bytes=64)
+                scales[i] = grp.tile([P, N], U8, name="s", align_bytes=64)
             nc.vector.quantize_mx(
-                out=codes[i, c][:].bitcast(FP8X4),
-                scales=scales[i, c][:],
-                in_=grouped[i, c][:].rearrange("p w j -> p (w j)"),
+                out=codes[i][:, c0:c1].bitcast(FP8X4),
+                scales=scales[i][:, c0:c1],
+                in_=grouped[i][:, c0:c1, :].rearrange("p w j -> p (w j)"),
             )
 
         def mm(i, c):
+            cols = slice(c * HALF, (c + 1) * HALF)
             nc.tensor.matmul_mx(
                 out=acc[c][:],
                 lhsT=x_codes[:, i, :].bitcast(FP8X4),
                 lhsT_scale=x_scales[:, i, :],
-                rhs=codes[i, c][:].bitcast(FP8X4),
-                rhs_scale=scales[i, c][:],
+                rhs=codes[i][:, cols].bitcast(FP8X4),
+                rhs_scale=scales[i][:, cols],
                 start=(i == 0),
                 stop=(i == PASSES - 1),
             )
-
-        xt = {}
-        gx = {}
 
         def xpose(s):
             words = x_sb[:, s, :].bitcast(F32)
@@ -139,82 +158,81 @@ def tile_snn_kernel(tc, FF, V, a, Xd, W_int, W_ff, out_0, out_1):
                 in_=gx[s][:].rearrange("p h r u -> p (h r u)").bitcast(BF16),
             )
 
-        load_w(0, chunks=4)
-        load_x(0)
-        load_w(1)
-        load_x(1)
-        load_w(2)
         nc.sync.dma_start(out=a_sb[:], in_=a)
         nc.sync.dma_start(out=v_sb[:], in_=V)
-        load_w(3)
-        for i in range(4, RAW_BUFS):
+        mid = 768
+        load_w(0, pieces=((HALF, mid), (mid, N)))
+        load_x(0)
+        load_w_piece(0, 0, HALF)
+        load_x(1)
+        load_w(1)
+        for i in range(2, RAW_BUFS):
             if i % 2 == 0:
-                load_x(i // 2)
+                load_x(i // 2 + 1)
             load_w(i)
 
-        alloc_grouped(0)
-        copy_cols("v", 0, 0, 256)
-        copy_cols("s", 0, 512, 768)
-        copy_cols("v", 0, 256, 512)
-        copy_cols("s", 0, 768, 1024)
-        xpose(0)
-        xcopy(0)
-        xquant(0)
+        nc.vector.scalar_tensor_tensor(
+            out=t_sb[:], in0=a_sb[:], scalar=-1.8, in1=v_sb[:], op0=ALU.mult, op1=ALU.add
+        )
+        nc.vector.tensor_scalar(out=x_out[:], in0=t_sb[:], scalar1=1.0, scalar2=None, op0=ALU.is_gt)
+        nc.vector.scalar_tensor_tensor(
+            out=a_out[:], in0=a_sb[:], scalar=0.9, in1=x_out[:], op0=ALU.mult, op1=ALU.add
+        )
+        nc.vector.scalar_tensor_tensor(
+            out=v_keep[:], in0=t_sb[:], scalar=1.0, in1=v_sb[:], op0=ALU.is_le, op1=ALU.mult
+        )
 
-        def elementwise(step):
-            if step == 2:
-                nc.vector.scalar_tensor_tensor(
-                    out=t_sb[:], in0=a_sb[:], scalar=-1.8, in1=v_sb[:], op0=ALU.mult, op1=ALU.add
-                )
-            if step == 3:
-                nc.vector.tensor_scalar(
-                    out=x_out[:], in0=t_sb[:], scalar1=1.0, scalar2=None, op0=ALU.is_gt
-                )
-                nc.sync.dma_start(out=out_0[0], in_=x_out[:])
-            if step == 4:
-                nc.vector.scalar_tensor_tensor(
-                    out=a_out[:], in0=a_sb[:], scalar=0.9, in1=x_out[:], op0=ALU.mult, op1=ALU.add
-                )
-                nc.sync.dma_start(out=out_0[2], in_=a_out[:])
-                nc.scalar.activation(
-                    out=x_f8[:], in_=x_out[:], func=ACT.Copy, scale=Y_SCALE, saturate=False
-                )
-                nc.sync.dma_start(out=out_1[0], in_=x_f8[:].bitcast(U8))
-            if step == 5:
-                nc.vector.scalar_tensor_tensor(
-                    out=v_keep[:], in0=t_sb[:], scalar=1.0, in1=v_sb[:], op0=ALU.is_le, op1=ALU.mult
-                )
-                nc.scalar.activation(
-                    out=a_f8[:], in_=a_out[:], func=ACT.Copy, scale=Y_SCALE, saturate=False
-                )
-                nc.sync.dma_start(out=out_1[2], in_=a_f8[:].bitcast(U8))
+        alloc_pass(0)
+        copy_cols("s", 0, CV, mid)
+        copy_cols("s", 0, mid, N)
+        xpose(0)
+        xpose(1)
+        xcopy(0)
+        nc.scalar.activation(out=x_f8[:], in_=x_out[:], func=ACT.Copy, scale=Y_SCALE, saturate=False)
+        nc.scalar.activation(out=a_f8[:], in_=a_out[:], func=ACT.Copy, scale=Y_SCALE, saturate=False)
+        copy_cols("v", 0, 0, CV)
 
         for i in range(PASSES):
             nxt = i + 1
+            if PE_FROM <= nxt + 1 < PASSES:
+                pe_interleave(nxt + 1)
+            if nxt < PE_FROM:
+                alloc_pass(nxt)
+                copy_cols("v", nxt, 0, CV)
+                copy_cols("s", nxt, CV, N)
+            elif nxt < PASSES:
+                cv = CV_LAST if nxt == PASSES - 1 else CV_PE
+                alloc_pass(nxt)
+                copy_cols("v", nxt, 0, cv)
+                copy_cols("s", nxt, cv, N - PE_COLS)
+                pe_collect(nxt)
             if nxt < PASSES:
-                alloc_grouped(nxt)
-                if nxt == PASSES - 1:
-                    copy_cols("v", nxt, 0, 512)
-                    copy_cols("s", nxt, 512, 768)
-                    copy_cols("v", nxt, 768, 1024)
-                else:
-                    copy_cols("v", nxt, 0, 512)
-                    copy_cols("s", nxt, 512, 1024)
-                if nxt + RAW_BUFS - 1 < PASSES:
-                    j = nxt + RAW_BUFS - 1
-                    if j % 2 == 0:
-                        load_x(j // 2)
+                j = nxt + RAW_BUFS - 1
+                if j < PASSES:
+                    if j % 2 == 0 and j // 2 + 1 < GROUPS:
+                        load_x(j // 2 + 1)
                     load_w(j)
-            if i % 2 == 0 and i // 2 + 1 < GROUPS:
-                xpose(i // 2 + 1)
-                xcopy(i // 2 + 1)
-            quant(i, 0)
+                    if j == PASSES - 1:
+                        nc.sync.dma_start(out=out_0[0], in_=x_out[:])
+                        nc.sync.dma_start(out=out_0[2], in_=a_out[:])
+                        nc.sync.dma_start(out=out_1[0], in_=x_f8[:].bitcast(U8))
+                        nc.sync.dma_start(out=out_1[2], in_=a_f8[:].bitcast(U8))
+            if nxt % 2 == 1 and (nxt + 1) // 2 < GROUPS:
+                xcopy((nxt + 1) // 2)
+            if i == 0:
+                xquant(0)
+            if i < PASSES - 1:
+                quant(i, 0, N)
+            else:
+                quant(i, 0, HALF)
             mm(i, 0)
-            quant(i, 1)
+            if i == PASSES - 1:
+                quant(i, HALF, N)
             mm(i, 1)
-            if i % 2 == 1 and i // 2 + 1 < GROUPS:
-                xquant(i // 2 + 1)
-            elementwise(i)
+            if i % 2 == 1 and (i + 3) // 2 < GROUPS:
+                xpose((i + 3) // 2)
+            if i % 2 == 1 and (i + 1) // 2 < GROUPS:
+                xquant((i + 1) // 2)
 
         for c in range(2):
             cols = slice(c * HALF, (c + 1) * HALF)

@@ -21,9 +21,8 @@ GROUPS = 9
 PASSES = 18
 RAW_BUFS = 12
 Y_SCALE = 190.0
-CV = 528
-CV_PE = 488
-CV_LAST = 512
+CV = 536
+CV_PE = {11: 464, 12: 464, 13: 464, 14: 464, 15: 432, 16: 400, 17: 512}
 PE_FROM = 11
 PE_COLS = 256
 
@@ -164,11 +163,11 @@ def tile_snn_kernel(tc, FF, V, a, Xd, W_int, W_ff, out_0, out_1):
         load_w(0, pieces=((HALF, mid), (mid, N)))
         load_x(0)
         load_w_piece(0, 0, HALF)
-        load_x(1)
         load_w(1)
+        load_x(1)
         for i in range(2, RAW_BUFS):
-            if i % 2 == 0:
-                load_x(i // 2 + 1)
+            if i % 2 == 1:
+                load_x((i + 1) // 2)
             load_w(i)
 
         nc.vector.scalar_tensor_tensor(
@@ -201,7 +200,7 @@ def tile_snn_kernel(tc, FF, V, a, Xd, W_int, W_ff, out_0, out_1):
                 copy_cols("v", nxt, 0, CV)
                 copy_cols("s", nxt, CV, N)
             elif nxt < PASSES:
-                cv = CV_LAST if nxt == PASSES - 1 else CV_PE
+                cv = CV_PE[nxt]
                 alloc_pass(nxt)
                 copy_cols("v", nxt, 0, cv)
                 copy_cols("s", nxt, cv, N - PE_COLS)
@@ -209,8 +208,8 @@ def tile_snn_kernel(tc, FF, V, a, Xd, W_int, W_ff, out_0, out_1):
             if nxt < PASSES:
                 j = nxt + RAW_BUFS - 1
                 if j < PASSES:
-                    if j % 2 == 0 and j // 2 + 1 < GROUPS:
-                        load_x(j // 2 + 1)
+                    if j % 2 == 1 and (j + 1) // 2 < GROUPS:
+                        load_x((j + 1) // 2)
                     load_w(j)
                     if j == PASSES - 1:
                         nc.sync.dma_start(out=out_0[0], in_=x_out[:])

@@ -21,8 +21,8 @@ GROUPS = 9
 PASSES = 18
 RAW_BUFS = 12
 Y_SCALE = 190.0
-CV = 536
-CV_PE = {11: 464, 12: 464, 13: 464, 14: 464, 15: 432, 16: 400, 17: 512}
+CV = 552
+CV_PE = {11: 496, 12: 496, 13: 496, 14: 496, 15: 496, 16: 496, 17: 512}
 PE_FROM = 11
 PE_COLS = 256
 
@@ -90,12 +90,14 @@ def tile_snn_kernel(tc, FF, V, a, Xd, W_int, W_ff, out_0, out_1):
             nc.sync.dma_start(out=x_sb[:, s, :], in_=x_rows(s))
 
         def copy_cols(eng, i, c0, c1):
-            dst = grouped[i][:, c0:c1, :].rearrange("p (c i) t -> p c t i", i=4)
-            src = raw[i][:, :, c0:c1].rearrange("p t (c i) -> p c t i", i=4)
             if eng == "v":
+                dst = grouped[i][:, c0:c1, :].rearrange("p (c i) t -> p c t i", i=4)
+                src = raw[i][:, :, c0:c1].rearrange("p t (c i) -> p c t i", i=4)
                 nc.vector.tensor_copy(out=dst, in_=src)
             else:
-                nc.scalar.copy(out=dst, in_=src)
+                nc.scalar.copy(
+                    out=grouped[i][:, c0:c1, :], in_=raw[i][:, :, c0:c1].rearrange("p t c -> p c t")
+                )
 
         pw = {}
 

@@ -25,6 +25,8 @@ CV = 552
 CV_PE = {11: 496, 12: 496, 13: 496, 14: 496, 15: 496, 16: 496, 17: 512}
 PE_FROM = 11
 PE_COLS = 256
+GROUPS_OF_COLS = ((0, 512), (512, 768), (768, 1024))
+PIECES_FROM = 16
 
 
 def tile_snn_kernel(tc, FF, V, a, Xd, W_int, W_ff, out_0, out_1):
@@ -69,7 +71,7 @@ def tile_snn_kernel(tc, FF, V, a, Xd, W_int, W_ff, out_0, out_1):
         x_f8 = keep.tile([P, N], FP8, name="x_f8")
         a_f8 = keep.tile([P, N], FP8, name="a_f8")
         v_f8 = keep.tile([P, N], FP8, name="v_f8")
-        acc = [accp.tile([P, HALF], F32, name="acc%d" % c) for c in range(2)]
+        acc = [accp.tile([P, HALF], F32, name="acc%d" % c) for c in range(3)]
 
         raw = {}
         grouped = {}
@@ -128,9 +130,9 @@ def tile_snn_kernel(tc, FF, V, a, Xd, W_int, W_ff, out_0, out_1):
             )
 
         def mm(i, c):
-            cols = slice(c * HALF, (c + 1) * HALF)
+            cols = slice(GROUPS_OF_COLS[c][0], GROUPS_OF_COLS[c][1])
             nc.tensor.matmul_mx(
-                out=acc[c][:],
+                out=acc[c][:, 0 : cols.stop - cols.start],
                 lhsT=x_codes[:, i, :].bitcast(FP8X4),
                 lhsT_scale=x_scales[:, i, :],
                 rhs=codes[i][:, cols].bitcast(FP8X4),
@@ -222,27 +224,44 @@ def tile_snn_kernel(tc, FF, V, a, Xd, W_int, W_ff, out_0, out_1):
                 xcopy((nxt + 1) // 2)
             if i == 0:
                 xquant(0)
-            if i < PASSES - 1:
+            if i < PIECES_FROM:
                 quant(i, 0, N)
-            else:
-                quant(i, 0, HALF)
-            mm(i, 0)
-            if i == PASSES - 1:
+                mm(i, 0)
+                mm(i, 1)
+                mm(i, 2)
+            elif i < PASSES - 1:
                 quant(i, HALF, N)
-            mm(i, 1)
+                mm(i, 1)
+                mm(i, 2)
+            else:
+                quant(i, HALF, 768)
+                mm(i, 1)
+                quant(i, 768, N)
+                mm(i, 2)
             if i % 2 == 1 and (i + 3) // 2 < GROUPS:
                 xpose((i + 3) // 2)
             if i % 2 == 1 and (i + 1) // 2 < GROUPS:
                 xquant((i + 1) // 2)
+            if PIECES_FROM <= nxt < PASSES:
+                quant(nxt, 0, HALF)
+                mm(nxt, 0)
 
-        for c in range(2):
-            cols = slice(c * HALF, (c + 1) * HALF)
+        for c in range(3):
+            c0, c1 = GROUPS_OF_COLS[c]
             nc.vector.scalar_tensor_tensor(
-                out=v_out[:, cols], in0=v_keep[:, cols], scalar=0.95, in1=acc[c][:],
+                out=v_out[:, c0:c1], in0=v_keep[:, c0:c1], scalar=0.95, in1=acc[c][:, 0 : c1 - c0],
                 op0=ALU.mult, op1=ALU.add,
             )
-            nc.sync.dma_start(out=out_0[1][:, cols], in_=v_out[:, cols])
-            nc.scalar.activation(
-                out=v_f8[:, cols], in_=v_out[:, cols], func=ACT.Copy, scale=Y_SCALE, saturate=False
-            )
-            nc.sync.dma_start(out=out_1[1][:, cols], in_=v_f8[:, cols].bitcast(U8))
+            if c < 2:
+                nc.scalar.activation(
+                    out=v_f8[:, c0:c1], in_=v_out[:, c0:c1], func=ACT.Copy, scale=Y_SCALE, saturate=False
+                )
+            else:
+                nc.vector.tensor_scalar(
+                    out=v_f8[:, c0:c1], in0=v_out[:, c0:c1], scalar1=Y_SCALE, scalar2=None, op0=ALU.mult,
+                    saturate=False,
+                )
+            if c != 1:
+                nc.sync.dma_start(out=out_0[1][:, c1 - HALF : c1], in_=v_out[:, c1 - HALF : c1])
+        for c1 in (HALF, N):
+            nc.sync.dma_start(out=out_1[1][:, c1 - HALF : c1], in_=v_f8[:, c1 - HALF : c1].bitcast(U8))

@@ -21,8 +21,8 @@ GROUPS = 9
 PASSES = 18
 RAW_BUFS = 12
 Y_SCALE = 190.0
-CV = 552
-CV_PE = {11: 496, 12: 496, 13: 496, 14: 496, 15: 496, 16: 496, 17: 512}
+CV = 536
+CV_PE = {11: 480, 12: 480, 13: 480, 14: 480, 15: 480, 16: 480, 17: 512}
 PE_FROM = 11
 PE_COLS = 256
 GROUPS_OF_COLS = ((0, 512), (512, 768), (768, 1024))

@@ -22,10 +22,11 @@ PASSES = 18
 RAW_BUFS = 12
 Y_SCALE = 190.0
 CV = 536
-CV_PE = {11: 480, 12: 480, 13: 480, 14: 480, 15: 480, 16: 480, 17: 512}
+CV_PE = {11: 480, 12: 480, 13: 480, 14: 480, 15: 480, 16: 400, 17: 400}
 PE_FROM = 11
 PE_COLS = 256
 GROUPS_OF_COLS = ((0, 512), (512, 768), (768, 1024))
+X_BEFORE_W = {3: 2, 5: 3, 7: 4, 8: 5, 9: 6, 11: 7, 13: 8}
 PIECES_FROM = 16
 
 
@@ -141,6 +142,9 @@ def tile_snn_kernel(tc, FF, V, a, Xd, W_int, W_ff, out_0, out_1):
                 stop=(i == PASSES - 1),
             )
 
+        def lead(s):
+            return min(max(s - 4, 0), 2)
+
         def xpose(s):
             words = x_sb[:, s, :].bitcast(F32)
             xt[s] = xtp.tile([P, 2, 2, P], F32, name="xt")
@@ -170,8 +174,8 @@ def tile_snn_kernel(tc, FF, V, a, Xd, W_int, W_ff, out_0, out_1):
         load_w(1)
         load_x(1)
         for i in range(2, RAW_BUFS):
-            if i % 2 == 1:
-                load_x((i + 1) // 2)
+            if i in X_BEFORE_W:
+                load_x(X_BEFORE_W[i])
             load_w(i)
 
         nc.vector.scalar_tensor_tensor(
@@ -207,21 +211,26 @@ def tile_snn_kernel(tc, FF, V, a, Xd, W_int, W_ff, out_0, out_1):
                 cv = CV_PE[nxt]
                 alloc_pass(nxt)
                 copy_cols("v", nxt, 0, cv)
-                copy_cols("s", nxt, cv, N - PE_COLS)
+                if nxt >= PIECES_FROM and cv < HALF:
+                    copy_cols("s", nxt, cv, HALF)
+                    copy_cols("s", nxt, HALF, N - PE_COLS)
+                else:
+                    copy_cols("s", nxt, cv, N - PE_COLS)
                 pe_collect(nxt)
             if nxt < PASSES:
                 j = nxt + RAW_BUFS - 1
                 if j < PASSES:
-                    if j % 2 == 1 and (j + 1) // 2 < GROUPS:
-                        load_x((j + 1) // 2)
+                    if j in X_BEFORE_W:
+                        load_x(X_BEFORE_W[j])
                     load_w(j)
                     if j == PASSES - 1:
                         nc.sync.dma_start(out=out_0[0], in_=x_out[:])
                         nc.sync.dma_start(out=out_0[2], in_=a_out[:])
                         nc.sync.dma_start(out=out_1[0], in_=x_f8[:].bitcast(U8))
                         nc.sync.dma_start(out=out_1[2], in_=a_f8[:].bitcast(U8))
-            if nxt % 2 == 1 and (nxt + 1) // 2 < GROUPS:
-                xcopy((nxt + 1) // 2)
+            for s in range(1, GROUPS):
+                if 2 * s - 2 - lead(s) == i:
+                    xcopy(s)
             if i == 0:
                 xquant(0)
             if i < PIECES_FROM:
@@ -238,10 +247,12 @@ def tile_snn_kernel(tc, FF, V, a, Xd, W_int, W_ff, out_0, out_1):
                 mm(i, 1)
                 quant(i, 768, N)
                 mm(i, 2)
-            if i % 2 == 1 and (i + 3) // 2 < GROUPS:
-                xpose((i + 3) // 2)
-            if i % 2 == 1 and (i + 1) // 2 < GROUPS:
-                xquant((i + 1) // 2)
+            for s in range(2, GROUPS):
+                if 2 * s - 3 - lead(s) == i:
+                    xpose(s)
+            for s in range(1, GROUPS):
+                if 2 * s - 1 - lead(s) == i:
+                    xquant(s)
             if PIECES_FROM <= nxt < PASSES:
                 quant(nxt, 0, HALF)
                 mm(nxt, 0)

@@ -93,14 +93,12 @@ def tile_snn_kernel(tc, FF, V, a, Xd, W_int, W_ff, out_0, out_1):
             nc.sync.dma_start(out=x_sb[:, s, :], in_=x_rows(s))
 
         def copy_cols(eng, i, c0, c1):
+            dst = grouped[i][:, c0:c1, :].rearrange("p (c i) t -> p c t i", i=4)
+            src = raw[i][:, :, c0:c1].rearrange("p t (c i) -> p c t i", i=4)
             if eng == "v":
-                dst = grouped[i][:, c0:c1, :].rearrange("p (c i) t -> p c t i", i=4)
-                src = raw[i][:, :, c0:c1].rearrange("p t (c i) -> p c t i", i=4)
                 nc.vector.tensor_copy(out=dst, in_=src)
             else:
-                nc.scalar.copy(
-                    out=grouped[i][:, c0:c1, :], in_=raw[i][:, :, c0:c1].rearrange("p t c -> p c t")
-                )
+                nc.scalar.copy(out=dst, in_=src)
 
         pw = {}
 

from contextlib import ExitStack

import concourse.mybir as mybir
from concourse.masks import make_identity

FLOPS = 2 * 128 * 9216 * 1024

F32 = mybir.dt.float32
BF16 = mybir.dt.bfloat16
U32 = mybir.dt.uint32
U8 = mybir.dt.uint8
FP8X4 = mybir.dt.float8_e4m3fn_x4
FP8 = mybir.dt.float8_e4m3fn
ALU = mybir.AluOpType
ACT = mybir.ActivationFunctionType

P = 128
N = 1024
HALF = 512
GROUPS = 9
PASSES = 18
RAW_BUFS = 12
Y_SCALE = 190.0
CV = 536
CV_PE = {11: 480, 12: 480, 13: 480, 14: 480, 15: 480, 16: 400, 17: 400}
PE_FROM = 11
PE_COLS = 256
GROUPS_OF_COLS = ((0, 512), (512, 768), (768, 1024))
X_BEFORE_W = {3: 2, 5: 3, 7: 4, 8: 5, 9: 6, 11: 7, 13: 8}
PIECES_FROM = 16


def tile_snn_kernel(tc, FF, V, a, Xd, W_int, W_ff, out_0, out_1):
    nc = tc.nc

    def w_rows(i):
        s, h = divmod(i, 2)
        src = W_int[s] if s < 8 else W_ff
        return src[HALF * h : HALF * (h + 1), :].rearrange("(p j) w -> p j w", j=4)

    def x_rows(s):
        return Xd[s] if s < 8 else FF

    with ExitStack() as ctx:
        keep = ctx.enter_context(tc.tile_pool(name="keep", bufs=1))
        rawp = ctx.enter_context(tc.tile_pool(name="rawp", bufs=RAW_BUFS))
        grp = ctx.enter_context(tc.tile_pool(name="grp", bufs=3))
        accp = ctx.enter_context(tc.psum_pool(name="accp", bufs=1))
        xtp = ctx.enter_context(tc.psum_pool(name="xtp", bufs=2))
        pwp = ctx.enter_context(tc.psum_pool(name="pwp", bufs=3))
        ctx.enter_context(tc.manual_schedule())

        ident = keep.tile([P, P], F32, name="ident")
        make_identity(nc, ident[:])
        ident_bf = keep.tile([P, P], BF16, name="ident_bf")
        make_identity(nc, ident_bf[:])
        warm_in = keep.tile([P, 8], F32, name="warm_in")
        warm_out = keep.tile([P, 8], F32, name="warm_out")
        nc.gpsimd.memset(warm_in[:], 0.0)
        nc.scalar.activation(out=warm_out[:], in_=warm_in[:], func=ACT.Copy)

        x_sb = keep.tile([P, GROUPS, N], BF16, name="x_sb")
        x_codes = keep.tile([P, PASSES, P], U32, name="x_codes", align_bytes=64)
        x_scales = keep.tile([P, PASSES, P], U8, name="x_scales", align_bytes=64)
        a_sb = keep.tile([P, N], BF16, name="a_sb")
        v_sb = keep.tile([P, N], BF16, name="v_sb")
        t_sb = keep.tile([P, N], F32, name="t_sb")
        x_out = keep.tile([P, N], F32, name="x_out")
        a_out = keep.tile([P, N], F32, name="a_out")
        v_keep = keep.tile([P, N], F32, name="v_keep")
        v_out = keep.tile([P, N], F32, name="v_out")
        x_f8 = keep.tile([P, N], FP8, name="x_f8")
        a_f8 = keep.tile([P, N], FP8, name="a_f8")
        v_f8 = keep.tile([P, N], FP8, name="v_f8")
        acc = [accp.tile([P, HALF], F32, name="acc%d" % c) for c in range(3)]

        raw = {}
        grouped = {}
        codes = {}
        scales = {}
        xt = {}
        gx = {}

        def load_w(i, pieces=((0, N),)):
            raw[i] = rawp.tile([P, 4, N], BF16, name="raw")
            for c0, c1 in pieces:
                nc.sync.dma_start(out=raw[i][:, :, c0:c1], in_=w_rows(i)[:, :, c0:c1])

        def load_w_piece(i, c0, c1):
            nc.sync.dma_start(out=raw[i][:, :, c0:c1], in_=w_rows(i)[:, :, c0:c1])

        def load_x(s):
            nc.sync.dma_start(out=x_sb[:, s, :], in_=x_rows(s))

        def copy_cols(eng, i, c0, c1):
            dst = grouped[i][:, c0:c1, :].rearrange("p (c i) t -> p c t i", i=4)
            src = raw[i][:, :, c0:c1].rearrange("p t (c i) -> p c t i", i=4)
            if eng == "v":
                nc.vector.tensor_copy(out=dst, in_=src)
            else:
                nc.scalar.copy(out=dst, in_=src)

        pw = {}

        def pe_interleave(i):
            pw[i] = pwp.tile([P, PE_COLS, 4], BF16, name="pw")
            for j in (0, 2):
                nc.tensor.matmul(
                    out=pw[i][:, :, j : j + 2],
                    lhsT=ident_bf[:],
                    rhs=raw[i][:, j : j + 2, N - PE_COLS : N].rearrange("p j c -> p c j"),
                    start=True, stop=True,
                )

        def pe_collect(i):
            nc.scalar.copy(out=grouped[i][:, N - PE_COLS : N, :], in_=pw[i][:])

        def alloc_pass(i):
            grouped[i] = grp.tile([P, N, 4], BF16, name="g", align_bytes=64)

        def quant(i, c0, c1):
            if c0 == 0:
                codes[i] = grp.tile([P, N], U32, name="c", align_bytes=64)
                scales[i] = grp.tile([P, N], U8, name="s", align_bytes=64)
            nc.vector.quantize_mx(
                out=codes[i][:, c0:c1].bitcast(FP8X4),
                scales=scales[i][:, c0:c1],
                in_=grouped[i][:, c0:c1, :].rearrange("p w j -> p (w j)"),
            )

        def mm(i, c):
            cols = slice(GROUPS_OF_COLS[c][0], GROUPS_OF_COLS[c][1])
            nc.tensor.matmul_mx(
                out=acc[c][:, 0 : cols.stop - cols.start],
                lhsT=x_codes[:, i, :].bitcast(FP8X4),
                lhsT_scale=x_scales[:, i, :],
                rhs=codes[i][:, cols].bitcast(FP8X4),
                rhs_scale=scales[i][:, cols],
                start=(i == 0),
                stop=(i == PASSES - 1),
            )

        def lead(s):
            return min(max(s - 4, 0), 2)

        def xpose(s):
            words = x_sb[:, s, :].bitcast(F32)
            xt[s] = xtp.tile([P, 2, 2, P], F32, name="xt")
            for h in range(2):
                for u in range(2):
                    nc.tensor.transpose(
                        xt[s][:, h, u, :], words[:, 256 * h + u : 256 * (h + 1) : 2], ident[:]
                    )

        def xcopy(s):
            gx[s] = grp.tile([P, 2, P, 2], F32, name="gx", align_bytes=64)
            nc.scalar.copy(out=gx[s][:], in_=xt[s][:].rearrange("p h u r -> p h r u"))

        def xquant(s):
            nc.vector.quantize_mx(
                out=x_codes[:, 2 * s : 2 * s + 2, :].rearrange("p a m -> p (a m)").bitcast(FP8X4),
                scales=x_scales[:, 2 * s : 2 * s + 2, :].rearrange("p a m -> p (a m)"),
                in_=gx[s][:].rearrange("p h r u -> p (h r u)").bitcast(BF16),
            )

        nc.sync.dma_start(out=a_sb[:], in_=a)
        nc.sync.dma_start(out=v_sb[:], in_=V)
        mid = 768
        load_w(0, pieces=((HALF, mid), (mid, N)))
        load_x(0)
        load_w_piece(0, 0, HALF)
        load_w(1)
        load_x(1)
        for i in range(2, RAW_BUFS):
            if i in X_BEFORE_W:
                load_x(X_BEFORE_W[i])
            load_w(i)

        nc.vector.scalar_tensor_tensor(
            out=t_sb[:], in0=a_sb[:], scalar=-1.8, in1=v_sb[:], op0=ALU.mult, op1=ALU.add
        )
        nc.vector.tensor_scalar(out=x_out[:], in0=t_sb[:], scalar1=1.0, scalar2=None, op0=ALU.is_gt)
        nc.vector.scalar_tensor_tensor(
            out=a_out[:], in0=a_sb[:], scalar=0.9, in1=x_out[:], op0=ALU.mult, op1=ALU.add
        )
        nc.vector.scalar_tensor_tensor(
            out=v_keep[:], in0=t_sb[:], scalar=1.0, in1=v_sb[:], op0=ALU.is_le, op1=ALU.mult
        )

        alloc_pass(0)
        copy_cols("s", 0, CV, mid)
        copy_cols("s", 0, mid, N)
        xpose(0)
        xpose(1)
        xcopy(0)
        nc.scalar.activation(out=x_f8[:], in_=x_out[:], func=ACT.Copy, scale=Y_SCALE, saturate=False)
        nc.scalar.activation(out=a_f8[:], in_=a_out[:], func=ACT.Copy, scale=Y_SCALE, saturate=False)
        copy_cols("v", 0, 0, CV)

        for i in range(PASSES):
            nxt = i + 1
            if PE_FROM <= nxt + 1 < PASSES:
                pe_interleave(nxt + 1)
            if nxt < PE_FROM:
                alloc_pass(nxt)
                copy_cols("v", nxt, 0, CV)
                copy_cols("s", nxt, CV, N)
            elif nxt < PASSES:
                cv = CV_PE[nxt]
                alloc_pass(nxt)
                copy_cols("v", nxt, 0, cv)
                if nxt >= PIECES_FROM and cv < HALF:
                    copy_cols("s", nxt, cv, HALF)
                    copy_cols("s", nxt, HALF, N - PE_COLS)
                else:
                    copy_cols("s", nxt, cv, N - PE_COLS)
                pe_collect(nxt)
            if nxt < PASSES:
                j = nxt + RAW_BUFS - 1
                if j < PASSES:
                    if j in X_BEFORE_W:
                        load_x(X_BEFORE_W[j])
                    load_w(j)
                    if j == PASSES - 1:
                        nc.sync.dma_start(out=out_0[0], in_=x_out[:])
                        nc.sync.dma_start(out=out_0[2], in_=a_out[:])
                        nc.sync.dma_start(out=out_1[0], in_=x_f8[:].bitcast(U8))
                        nc.sync.dma_start(out=out_1[2], in_=a_f8[:].bitcast(U8))
            for s in range(1, GROUPS):
                if 2 * s - 2 - lead(s) == i:
                    xcopy(s)
            if i == 0:
                xquant(0)
            if i < PIECES_FROM:
                quant(i, 0, N)
                mm(i, 0)
                mm(i, 1)
                mm(i, 2)
            elif i < PASSES - 1:
                quant(i, HALF, N)
                mm(i, 1)
                mm(i, 2)
            else:
                quant(i, HALF, 768)
                mm(i, 1)
                quant(i, 768, N)
                mm(i, 2)
            for s in range(2, GROUPS):
                if 2 * s - 3 - lead(s) == i:
                    xpose(s)
            for s in range(1, GROUPS):
                if 2 * s - 1 - lead(s) == i:
                    xquant(s)
            if PIECES_FROM <= nxt < PASSES:
                quant(nxt, 0, HALF)
                mm(nxt, 0)

        for c in range(3):
            c0, c1 = GROUPS_OF_COLS[c]
            nc.vector.scalar_tensor_tensor(
                out=v_out[:, c0:c1], in0=v_keep[:, c0:c1], scalar=0.95, in1=acc[c][:, 0 : c1 - c0],
                op0=ALU.mult, op1=ALU.add,
            )
            if c < 2:
                nc.scalar.activation(
                    out=v_f8[:, c0:c1], in_=v_out[:, c0:c1], func=ACT.Copy, scale=Y_SCALE, saturate=False
                )
            else:
                nc.vector.tensor_scalar(
                    out=v_f8[:, c0:c1], in0=v_out[:, c0:c1], scalar1=Y_SCALE, scalar2=None, op0=ALU.mult,
                    saturate=False,
                )
            if c != 1:
                nc.sync.dma_start(out=out_0[1][:, c1 - HALF : c1], in_=v_out[:, c1 - HALF : c1])
        for c1 in (HALF, N):
            nc.sync.dma_start(out=out_1[1][:, c1 - HALF : c1], in_=v_f8[:, c1 - HALF : c1].bitcast(U8))
